import numpy as np
import ml_dtypes


def mxq(x, axis, fmt="e4m3"):
    dtype, down = {"e4m3": (ml_dtypes.float8_e4m3fn, 7), "e5m2": (ml_dtypes.float8_e5m2, 14)}[fmt]
    v = np.moveaxis(np.asarray(x, np.float32).astype(ml_dtypes.bfloat16).astype(np.float64), axis, -1)
    blocks = v.reshape(v.shape[:-1] + (-1, 32))
    amax = np.abs(blocks).max(-1, keepdims=True)
    byte = np.maximum(np.where(amax > 0, np.frexp(amax)[1] - 1 + 127, 0) - down, 1)
    scale = np.exp2(byte - 127.0)
    codes = (blocks / scale).astype(np.float32).astype(dtype).astype(np.float64)
    return np.moveaxis((codes * scale).reshape(v.shape), -1, axis)


WIDE = False


def mx_kscale(k):
    if not WIDE:
        return np.ones(k)
    levels = np.array([20, -20, 10, -10, 0])
    a = np.random.permutation(np.resize(levels, k // 512 * 4)).reshape(k // 512, 4)
    idx = np.arange(k)
    return np.exp2(a[idx // 512, idx % 128 // 32])


BF16 = ml_dtypes.bfloat16


def bf(x):
    return np.asarray(x, np.float32).astype(BF16)


def f64(x):
    return np.asarray(x).astype(np.float64)


B, IN, OUT, R, Q, ORD = 512, 1024, 1024, 8, 1024, 3
K = R ** ORD


def setup_inputs():
    s = mx_kscale(Q)[:, None]
    z = np.random.standard_normal((ORD, R, B))
    g2 = np.random.standard_normal((Q, K)) / np.sqrt(K) / s
    g = np.random.standard_normal((Q, B)) * np.exp2(np.random.randint(-12, 1, (1, B))) * s
    return {"z": bf(z), "G2": bf(g2), "grad_out": bf(g)}


def reference(z, G2, grad_out):
    Z = f64(z)
    dk = mxq(f64(G2), 0, "e4m3").T @ mxq(f64(grad_out), 0, "e5m2")
    D = dk.reshape((R, R, R, B))
    t = (D * Z[2][:, None, None, :]).sum(axis=0)
    d0 = (t * Z[1][:, None, :]).sum(axis=0)
    d1 = (t * Z[0][None, :, :]).sum(axis=1)
    u = (D * Z[0][None, None, :, :]).sum(axis=2)
    d2 = (u * Z[1][None, :, :]).sum(axis=1)
    return np.stack([d0, d1, d2], axis=0)

@@ -1,0 +1,206 @@
+from contextlib import ExitStack
+
+import concourse.mybir as mybir
+from concourse.masks import make_identity
+
+BF16 = mybir.dt.bfloat16
+F32 = mybir.dt.float32
+U32 = mybir.dt.uint32
+U8 = mybir.dt.uint8
+E4M3X4 = mybir.dt.float8_e4m3fn_x4
+E5M2X4 = mybir.dt.float8_e5m2_x4
+MULT = mybir.AluOpType.mult
+ADD = mybir.AluOpType.add
+AXIS_X = mybir.AxisListType.X
+
+P = 128
+PACK = 4
+K_PASS = P * PACK
+Q = 1024
+PASSES = Q // K_PASS
+ORD = 3
+R = 8
+KRON = R * R * R
+B = 512
+N_TILES = B // P
+RR = R * R
+
+FLOPS = 2 * Q * KRON * B + 2 * 2 * KRON * B + 3 * 2 * RR * B
+
+
+def regroup(nc, grouped, raw, first, vector_cols, scalar_cols):
+    shares = (
+        (nc.vector.tensor_copy, first, vector_cols),
+        (nc.scalar.copy, first + vector_cols, scalar_cols),
+    )
+    for copy, start, cols in shares:
+        if cols > 0:
+            copy(
+                out=grouped[:, start : start + cols, :].rearrange("p (w i) t -> p w t i", i=4),
+                in_=raw[:, :, start : start + cols].rearrange("p t (w i) -> p w t i", i=4),
+            )
+
+
+def quantise(nc, fmt, codes, scales, grouped):
+    nc.vector.quantize_mx(
+        out=codes.bitcast(fmt),
+        scales=scales,
+        in_=grouped.rearrange("p w t -> p (w t)"),
+    )
+
+
+def tile_fast_tucker_taylor_pa_s_kernel(tc, z, G2, grad_out, out):
+    nc = tc.nc
+    with ExitStack() as ctx:
+        keep = ctx.enter_context(tc.tile_pool(name="keep", bufs=1))
+        psum = ctx.enter_context(tc.psum_pool(name="psum", bufs=1))
+
+        ident_bf = keep.tile([P, P], BF16)
+        make_identity(nc, ident_bf[:])
+        ident_f32 = keep.tile([P, P], F32)
+        make_identity(nc, ident_f32[:])
+
+        z_rows = keep.tile([P, P], BF16)
+        nc.vector.memset(z_rows[:], 0.0)
+        res = keep.tile([P, P], F32)
+        nc.vector.memset(res[:], 0.0)
+
+        nc.scalar.dma_start(
+            out=z_rows[0 : ORD * R * N_TILES, :],
+            in_=z.rearrange("i r (j n) -> (i r j) n", j=N_TILES),
+        )
+        raw_w = []
+        raw_g = []
+        for source, raws, label in ((G2, raw_w, "w"), (grad_out, raw_g, "g")):
+            for c in range(PASSES):
+                raw = keep.tile([P, PACK, 512], BF16, name="raw_%s%d" % (label, c))
+                nc.sync.dma_start(
+                    out=raw[:],
+                    in_=source[c * K_PASS : (c + 1) * K_PASS, :].rearrange(
+                        "(p t) w -> p t w", t=PACK
+                    ),
+                )
+                raws.append(raw)
+
+        zT_ps = psum.tile([P, P], BF16)
+        nc.tensor.transpose(zT_ps[:], z_rows[:], ident_bf[:])
+        zT = keep.tile([P, ORD, N_TILES, R], F32)
+        nc.scalar.copy(
+            out=zT[:],
+            in_=zT_ps[:, 0 : ORD * R * N_TILES].rearrange(
+                "p (i r j) -> p i j r", i=ORD, r=R
+            ),
+        )
+
+        w_codes = keep.tile([P, PASSES, KRON], U32, align_bytes=64)
+        w_scales = keep.tile([P, PASSES, KRON], U8, align_bytes=64)
+        g_codes = keep.tile([P, PASSES, B], U32, align_bytes=64)
+        g_scales = keep.tile([P, PASSES, B], U8, align_bytes=64)
+        grouped_w = []
+        grouped_g = []
+        for c in range(PASSES):
+            grouped_w.append(
+                keep.tile([P, KRON, PACK], BF16, align_bytes=64, name="grouped_w%d" % c)
+            )
+            grouped_g.append(
+                keep.tile([P, B, PACK], BF16, align_bytes=64, name="grouped_g%d" % c)
+            )
+
+        HALF = 256
+        regroup(nc, grouped_w[0], raw_w[0], 0, HALF, HALF)
+        regroup(nc, grouped_w[1], raw_w[1], 0, HALF, HALF)
+        quantise(nc, E4M3X4, w_codes[:, 0, :], w_scales[:, 0, :], grouped_w[0][:])
+        regroup(nc, grouped_g[0], raw_g[0], 0, HALF, HALF)
+        quantise(nc, E4M3X4, w_codes[:, 1, :], w_scales[:, 1, :], grouped_w[1][:])
+        regroup(nc, grouped_g[1], raw_g[1], 0, 176, 80)
+        quantise(nc, E5M2X4, g_codes[:, 0, :], g_scales[:, 0, :], grouped_g[0][:])
+        regroup(nc, grouped_g[1], raw_g[1], HALF, 0, HALF)
+
+        dT = []
+        for j in range(N_TILES):
+            dT.append(psum.tile([P, KRON], F32, name="dT%d" % j))
+
+        def mx_pass(j, c):
+            samples = slice(j * P, (j + 1) * P)
+            nc.tensor.matmul_mx(
+                out=dT[j][:],
+                lhsT=g_codes[:, c, samples].bitcast(E5M2X4),
+                lhsT_scale=g_scales[:, c, samples],
+                rhs=w_codes[:, c, :].bitcast(E4M3X4),
+                rhs_scale=w_scales[:, c, :],
+                start=(c == 0),
+                stop=(c == PASSES - 1),
+            )
+
+        for j in range(N_TILES):
+            mx_pass(j, 0)
+
+        tu = keep.tile([P, 2, N_TILES, RR], F32)
+
+        def contract_step(acc, d_slice, z_column, first):
+            if first:
+                nc.vector.tensor_scalar_mul(out=acc, in0=d_slice, scalar1=z_column)
+            else:
+                nc.vector.scalar_tensor_tensor(
+                    out=acc, in0=d_slice, scalar=z_column, in1=acc, op0=MULT, op1=ADD
+                )
+
+        for pair in range(N_TILES // 2):
+            cols = slice(pair * HALF, (pair + 1) * HALF)
+            quantise(
+                nc, E5M2X4, g_codes[:, 1, cols], g_scales[:, 1, cols], grouped_g[1][:, cols, :]
+            )
+            tiles = (2 * pair, 2 * pair + 1)
+            for j in tiles:
+                mx_pass(j, 1)
+            for s in range(R):
+                for j in tiles:
+                    contract_step(
+                        tu[:, 0, j, :], dT[j][:, s * RR : (s + 1) * RR], zT[:, 2, j, s : s + 1], s == 0
+                    )
+                    contract_step(
+                        tu[:, 1, j, :],
+                        dT[j][:].rearrange("p (cb a) -> p cb a", a=R)[:, :, s],
+                        zT[:, 0, j, s : s + 1],
+                        s == 0,
+                    )
+
+        prod0 = keep.tile([P, N_TILES, R, R], F32)
+        nc.vector.tensor_tensor(
+            out=prod0[:],
+            in0=tu[:, 0, :, :].rearrange("p j (b a) -> p j b a", a=R),
+            in1=zT[:, 1, :, :].unsqueeze(3).to_broadcast([P, N_TILES, R, R]),
+            op=MULT,
+        )
+        prod12 = keep.tile([P, 2 * N_TILES, R, R], F32)
+        nc.vector.tensor_tensor(
+            out=prod12[:],
+            in0=tu[:].rearrange("p s j (x y) -> p (s j) x y", y=R),
+            in1=zT[:, 0:2, :, :]
+            .rearrange("p i j r -> p (i j) r")
+            .unsqueeze(2)
+            .to_broadcast([P, 2 * N_TILES, R, R]),
+            op=MULT,
+        )
+        res_view = res[:, 0 : ORD * R * N_TILES].rearrange("p (i r j) -> p i j r", i=ORD, r=R)
+        nc.vector.tensor_reduce(
+            out=res_view[:, 0, :, :],
+            in_=prod0[:].rearrange("p j b a -> p j a b"),
+            axis=AXIS_X,
+            op=ADD,
+        )
+        nc.vector.tensor_reduce(
+            out=res_view[:, 1:3, :, :],
+            in_=prod12[:].rearrange("p (s j) x y -> p s j x y", s=2),
+            axis=AXIS_X,
+            op=ADD,
+        )
+
+        resT_ps = psum.tile([P, P], F32)
+        nc.tensor.transpose(resT_ps[:], res[:], ident_f32[:])
+        resT = keep.tile([P, P], F32)
+        nc.scalar.copy(out=resT[:], in_=resT_ps[:])
+        nc.sync.dma_start(
+            out=out.rearrange("i r (j n) -> (i r j) n", j=N_TILES),
+            in_=resT[0 : ORD * R * N_TILES, :],
+        )

@@ -12,6 +12,7 @@ E5M2X4 = mybir.dt.float8_e5m2_x4
 MULT = mybir.AluOpType.mult
 ADD = mybir.AluOpType.add
 AXIS_X = mybir.AxisListType.X
+COPY = mybir.ActivationFunctionType.Copy
 
 P = 128
 PACK = 4
@@ -20,32 +21,22 @@ Q = 1024
 PASSES = Q // K_PASS
 ORD = 3
 R = 8
+RR = R * R
 KRON = R * R * R
 B = 512
 N_TILES = B // P
-RR = R * R
+Z_ROWS = ORD * R * N_TILES
+HALF = 256
+RUN = 4
+LAG = 1
 
 FLOPS = 2 * Q * KRON * B + 2 * 2 * KRON * B + 3 * 2 * RR * B
 
 
-def regroup(nc, grouped, raw, first, vector_cols, scalar_cols):
-    shares = (
-        (nc.vector.tensor_copy, first, vector_cols),
-        (nc.scalar.copy, first + vector_cols, scalar_cols),
-    )
-    for copy, start, cols in shares:
-        if cols > 0:
-            copy(
-                out=grouped[:, start : start + cols, :].rearrange("p (w i) t -> p w t i", i=4),
-                in_=raw[:, :, start : start + cols].rearrange("p t (w i) -> p w t i", i=4),
-            )
-
-
-def quantise(nc, fmt, codes, scales, grouped):
-    nc.vector.quantize_mx(
-        out=codes.bitcast(fmt),
-        scales=scales,
-        in_=grouped.rearrange("p w t -> p (w t)"),
+def regroup(copy, grouped, raw):
+    copy(
+        out=grouped.rearrange("p (w i) t -> p w t i", i=RUN),
+        in_=raw.rearrange("p t (w i) -> p w t i", i=RUN),
     )
 
 
@@ -54,26 +45,25 @@ def tile_fast_tucker_taylor_pa_s_kernel(tc, z, G2, grad_out, out):
     with ExitStack() as ctx:
         keep = ctx.enter_context(tc.tile_pool(name="keep", bufs=1))
         psum = ctx.enter_context(tc.psum_pool(name="psum", bufs=1))
+        ctx.enter_context(tc.manual_schedule())
 
+        z_rows = keep.tile([P, P], BF16)
+        nc.vector.memset(z_rows[:], 0.0)
+        nc.scalar.dma_start(
+            out=z_rows[0:Z_ROWS, :], in_=z.rearrange("i r (j n) -> (i r j) n", j=N_TILES)
+        )
         ident_bf = keep.tile([P, P], BF16)
         make_identity(nc, ident_bf[:])
         ident_f32 = keep.tile([P, P], F32)
         make_identity(nc, ident_f32[:])
-
-        z_rows = keep.tile([P, P], BF16)
-        nc.vector.memset(z_rows[:], 0.0)
         res = keep.tile([P, P], F32)
         nc.vector.memset(res[:], 0.0)
 
-        nc.scalar.dma_start(
-            out=z_rows[0 : ORD * R * N_TILES, :],
-            in_=z.rearrange("i r (j n) -> (i r j) n", j=N_TILES),
-        )
         raw_w = []
         raw_g = []
-        for source, raws, label in ((G2, raw_w, "w"), (grad_out, raw_g, "g")):
-            for c in range(PASSES):
-                raw = keep.tile([P, PACK, 512], BF16, name="raw_%s%d" % (label, c))
+        for c in range(PASSES):
+            for source, raws, label in ((G2, raw_w, "w"), (grad_out, raw_g, "g")):
+                raw = keep.tile([P, PACK, 2 * HALF], BF16, name="raw_%s%d" % (label, c))
                 nc.sync.dma_start(
                     out=raw[:],
                     in_=source[c * K_PASS : (c + 1) * K_PASS, :].rearrange(
@@ -82,58 +72,70 @@ def tile_fast_tucker_taylor_pa_s_kernel(tc, z, G2, grad_out, out):
                 )
                 raws.append(raw)
 
-        zT_ps = psum.tile([P, P], BF16)
-        nc.tensor.transpose(zT_ps[:], z_rows[:], ident_bf[:])
-        zT = keep.tile([P, ORD, N_TILES, R], F32)
-        nc.scalar.copy(
-            out=zT[:],
-            in_=zT_ps[:, 0 : ORD * R * N_TILES].rearrange(
-                "p (i r j) -> p i j r", i=ORD, r=R
-            ),
-        )
-
+        grouped_w = keep.tile([P, PASSES, KRON, PACK], BF16, align_bytes=64)
         w_codes = keep.tile([P, PASSES, KRON], U32, align_bytes=64)
         w_scales = keep.tile([P, PASSES, KRON], U8, align_bytes=64)
-        g_codes = keep.tile([P, PASSES, B], U32, align_bytes=64)
-        g_scales = keep.tile([P, PASSES, B], U8, align_bytes=64)
-        grouped_w = []
-        grouped_g = []
-        for c in range(PASSES):
-            grouped_w.append(
-                keep.tile([P, KRON, PACK], BF16, align_bytes=64, name="grouped_w%d" % c)
-            )
-            grouped_g.append(
-                keep.tile([P, B, PACK], BF16, align_bytes=64, name="grouped_g%d" % c)
-            )
+        grouped_g = keep.tile([P, 2, PASSES, HALF, PACK], BF16, align_bytes=64)
+        g_codes = keep.tile([P, 2, PASSES, HALF], U32, align_bytes=64)
+        g_scales = keep.tile([P, 2, PASSES, HALF], U8, align_bytes=64)
 
-        HALF = 256
-        regroup(nc, grouped_w[0], raw_w[0], 0, HALF, HALF)
-        regroup(nc, grouped_w[1], raw_w[1], 0, HALF, HALF)
-        quantise(nc, E4M3X4, w_codes[:, 0, :], w_scales[:, 0, :], grouped_w[0][:])
-        regroup(nc, grouped_g[0], raw_g[0], 0, HALF, HALF)
-        quantise(nc, E4M3X4, w_codes[:, 1, :], w_scales[:, 1, :], grouped_w[1][:])
-        regroup(nc, grouped_g[1], raw_g[1], 0, 176, 80)
-        quantise(nc, E5M2X4, g_codes[:, 0, :], g_scales[:, 0, :], grouped_g[0][:])
-        regroup(nc, grouped_g[1], raw_g[1], HALF, 0, HALF)
+        def quantise_w(c):
+            nc.vector.quantize_mx(
+                out=w_codes[:, c, :].bitcast(E4M3X4),
+                scales=w_scales[:, c, :],
+                in_=grouped_w[:, c, :, :].rearrange("p w t -> p (w t)"),
+            )
 
         dT = []
         for j in range(N_TILES):
             dT.append(psum.tile([P, KRON], F32, name="dT%d" % j))
 
         def mx_pass(j, c):
-            samples = slice(j * P, (j + 1) * P)
+            half = j // 2
+            samples = slice((j % 2) * P, (j % 2 + 1) * P)
             nc.tensor.matmul_mx(
                 out=dT[j][:],
-                lhsT=g_codes[:, c, samples].bitcast(E5M2X4),
-                lhsT_scale=g_scales[:, c, samples],
+                lhsT=g_codes[:, half, c, samples].bitcast(E5M2X4),
+                lhsT_scale=g_scales[:, half, c, samples],
                 rhs=w_codes[:, c, :].bitcast(E4M3X4),
                 rhs_scale=w_scales[:, c, :],
                 start=(c == 0),
                 stop=(c == PASSES - 1),
             )
 
-        for j in range(N_TILES):
-            mx_pass(j, 0)
+        def regroup_w(c):
+            regroup(nc.vector.tensor_copy, grouped_w[:, c, 0:HALF, :], raw_w[c][:, :, 0:HALF])
+            regroup(nc.scalar.copy, grouped_w[:, c, HALF:, :], raw_w[c][:, :, HALF:])
+
+        def regroup_g(c):
+            regroup(nc.vector.tensor_copy, grouped_g[:, 0, c, :, :], raw_g[c][:, :, 0:HALF])
+            regroup(nc.scalar.copy, grouped_g[:, 1, c, :, :], raw_g[c][:, :, HALF:])
+
+        def multiply_half(half, c):
+            nc.vector.quantize_mx(
+                out=g_codes[:, half, c, :].bitcast(E5M2X4),
+                scales=g_scales[:, half, c, :],
+                in_=grouped_g[:, half, c, :, :].rearrange("p w t -> p (w t)"),
+            )
+            mx_pass(2 * half, c)
+            mx_pass(2 * half + 1, c)
+
+        regroup_w(0)
+        regroup_g(0)
+        quantise_w(0)
+        multiply_half(0, 0)
+        regroup_w(1)
+        multiply_half(1, 0)
+        regroup_g(1)
+        zT_ps = psum.tile([P, P], BF16)
+        nc.tensor.transpose(zT_ps[:], z_rows[:], ident_bf[:])
+        zT = keep.tile([P, ORD, N_TILES, R], F32)
+        nc.scalar.copy(
+            out=zT[:], in_=zT_ps[:, 0:Z_ROWS].rearrange("p (i r j) -> p i j r", i=ORD, r=R)
+        )
+        quantise_w(1)
+        multiply_half(0, 1)
+        multiply_half(1, 1)
 
         tu = keep.tile([P, 2, N_TILES, RR], F32)
 
@@ -145,25 +147,33 @@ def tile_fast_tucker_taylor_pa_s_kernel(tc, z, G2, grad_out, out):
                     out=acc, in0=d_slice, scalar=z_column, in1=acc, op0=MULT, op1=ADD
                 )
 
-        for pair in range(N_TILES // 2):
-            cols = slice(pair * HALF, (pair + 1) * HALF)
-            quantise(
-                nc, E5M2X4, g_codes[:, 1, cols], g_scales[:, 1, cols], grouped_g[1][:, cols, :]
+        def d_slices(j, s):
+            return (
+                (dT[j][:, s * RR : (s + 1) * RR], zT[:, 2, j, s : s + 1]),
+                (dT[j][:].rearrange("p (cb a) -> p cb a", a=R)[:, :, s], zT[:, 0, j, s : s + 1]),
             )
-            tiles = (2 * pair, 2 * pair + 1)
-            for j in tiles:
-                mx_pass(j, 1)
-            for s in range(R):
-                for j in tiles:
-                    contract_step(
-                        tu[:, 0, j, :], dT[j][:, s * RR : (s + 1) * RR], zT[:, 2, j, s : s + 1], s == 0
-                    )
-                    contract_step(
-                        tu[:, 1, j, :],
-                        dT[j][:].rearrange("p (cb a) -> p cb a", a=R)[:, :, s],
-                        zT[:, 0, j, s : s + 1],
-                        s == 0,
-                    )
+
+        last = N_TILES - 1
+        terms = keep.tile([P, R, 2, RR], F32)
+        tu_last_ps = psum.tile([P, 2, RR], F32)
+        for s in range(R):
+            for k, (d_slice, z_column) in enumerate(d_slices(last, s)):
+                nc.scalar.activation(out=terms[:, s, k, :], in_=d_slice, func=COPY, scale=z_column)
+            nc.tensor.matmul(
+                out=tu_last_ps[:].rearrange("p k x -> p (k x)"),
+                lhsT=ident_f32[:],
+                rhs=terms[:, s, :, :].rearrange("p k x -> p (k x)"),
+                start=(s == 0),
+                stop=(s == R - 1),
+            )
+        nc.scalar.copy(out=tu[:, :, last, :], in_=tu_last_ps[:])
+
+        for turn in range(R + LAG):
+            for j in range(last):
+                s = turn - LAG if j == 2 else turn
+                if 0 <= s < R:
+                    for k, (d_slice, z_column) in enumerate(d_slices(j, s)):
+                        contract_step(tu[:, k, j, :], d_slice, z_column, s == 0)
 
         prod0 = keep.tile([P, N_TILES, R, R], F32)
         nc.vector.tensor_tensor(
@@ -182,7 +192,7 @@ def tile_fast_tucker_taylor_pa_s_kernel(tc, z, G2, grad_out, out):
             .to_broadcast([P, 2 * N_TILES, R, R]),
             op=MULT,
         )
-        res_view = res[:, 0 : ORD * R * N_TILES].rearrange("p (i r j) -> p i j r", i=ORD, r=R)
+        res_view = res[:, 0:Z_ROWS].rearrange("p (i r j) -> p i j r", i=ORD, r=R)
         nc.vector.tensor_reduce(
             out=res_view[:, 0, :, :],
             in_=prod0[:].rearrange("p j b a -> p j a b"),
@@ -201,6 +211,5 @@ def tile_fast_tucker_taylor_pa_s_kernel(tc, z, G2, grad_out, out):
         resT = keep.tile([P, P], F32)
         nc.scalar.copy(out=resT[:], in_=resT_ps[:])
         nc.sync.dma_start(
-            out=out.rearrange("i r (j n) -> (i r j) n", j=N_TILES),
-            in_=resT[0 : ORD * R * N_TILES, :],
+            out=out.rearrange("i r (j n) -> (i r j) n", j=N_TILES), in_=resT[0:Z_ROWS, :]
         )

@@ -26,6 +26,7 @@ KRON = R * R * R
 B = 512
 N_TILES = B // P
 Z_ROWS = ORD * R * N_TILES
+STORE_CUT = 64
 HALF = 256
 RUN = 4
 LAG = 1
@@ -210,6 +211,6 @@ def tile_fast_tucker_taylor_pa_s_kernel(tc, z, G2, grad_out, out):
         nc.tensor.transpose(resT_ps[:], res[:], ident_f32[:])
         resT = keep.tile([P, P], F32)
         nc.scalar.copy(out=resT[:], in_=resT_ps[:])
-        nc.sync.dma_start(
-            out=out.rearrange("i r (j n) -> (i r j) n", j=N_TILES), in_=resT[0:Z_ROWS, :]
-        )
+        out_rows = out.rearrange("i r (j n) -> (i r j) n", j=N_TILES)
+        nc.sync.dma_start(out=out_rows[0:STORE_CUT, :], in_=resT[0:STORE_CUT, :])
+        nc.sync.dma_start(out=out_rows[STORE_CUT:Z_ROWS, :], in_=resT[STORE_CUT:Z_ROWS, :])

@@ -28,7 +28,7 @@ N_TILES = B // P
 Z_ROWS = ORD * R * N_TILES
 STORE_CUT = 64
 HALF = 256
-RUN = 4
+RUN = 1
 LAG = 1
 
 FLOPS = 2 * Q * KRON * B + 2 * 2 * KRON * B + 3 * 2 * RR * B
@@ -80,11 +80,12 @@ def tile_fast_tucker_taylor_pa_s_kernel(tc, z, G2, grad_out, out):
         g_codes = keep.tile([P, 2, PASSES, HALF], U32, align_bytes=64)
         g_scales = keep.tile([P, 2, PASSES, HALF], U8, align_bytes=64)
 
-        def quantise_w(c):
+        def quantise_w(c, half):
+            columns = slice(half * HALF, (half + 1) * HALF)
             nc.vector.quantize_mx(
-                out=w_codes[:, c, :].bitcast(E4M3X4),
-                scales=w_scales[:, c, :],
-                in_=grouped_w[:, c, :, :].rearrange("p w t -> p (w t)"),
+                out=w_codes[:, c, columns].bitcast(E4M3X4),
+                scales=w_scales[:, c, columns],
+                in_=grouped_w[:, c, columns, :].rearrange("p w t -> p (w t)"),
             )
 
         dT = []
@@ -122,11 +123,13 @@ def tile_fast_tucker_taylor_pa_s_kernel(tc, z, G2, grad_out, out):
             mx_pass(2 * half + 1, c)
 
         regroup_w(0)
+        quantise_w(0, 0)
         regroup_g(0)
-        quantise_w(0)
+        quantise_w(0, 1)
         multiply_half(0, 0)
         regroup_w(1)
         multiply_half(1, 0)
+        quantise_w(1, 0)
         regroup_g(1)
         zT_ps = psum.tile([P, P], BF16)
         nc.tensor.transpose(zT_ps[:], z_rows[:], ident_bf[:])
@@ -134,7 +137,7 @@ def tile_fast_tucker_taylor_pa_s_kernel(tc, z, G2, grad_out, out):
         nc.scalar.copy(
             out=zT[:], in_=zT_ps[:, 0:Z_ROWS].rearrange("p (i r j) -> p i j r", i=ORD, r=R)
         )
-        quantise_w(1)
+        quantise_w(1, 1)
         multiply_half(0, 1)
         multiply_half(1, 1)
 

@@ -26,7 +26,7 @@ KRON = R * R * R
 B = 512
 N_TILES = B // P
 Z_ROWS = ORD * R * N_TILES
-STORE_CUT = 64
+BLOCK = 32
 HALF = 256
 RUN = 1
 LAG = 1
@@ -57,7 +57,7 @@ def tile_fast_tucker_taylor_pa_s_kernel(tc, z, G2, grad_out, out):
         make_identity(nc, ident_bf[:])
         ident_f32 = keep.tile([P, P], F32)
         make_identity(nc, ident_f32[:])
-        res = keep.tile([P, P], F32)
+        res = keep.tile([P, P], F32, align_bytes=64)
         nc.vector.memset(res[:], 0.0)
 
         raw_w = []
@@ -210,10 +210,16 @@ def tile_fast_tucker_taylor_pa_s_kernel(tc, z, G2, grad_out, out):
             op=ADD,
         )
 
-        resT_ps = psum.tile([P, P], F32)
-        nc.tensor.transpose(resT_ps[:], res[:], ident_f32[:])
-        resT = keep.tile([P, P], F32)
-        nc.scalar.copy(out=resT[:], in_=resT_ps[:])
-        out_rows = out.rearrange("i r (j n) -> (i r j) n", j=N_TILES)
-        nc.sync.dma_start(out=out_rows[0:STORE_CUT, :], in_=resT[0:STORE_CUT, :])
-        nc.sync.dma_start(out=out_rows[STORE_CUT:Z_ROWS, :], in_=resT[STORE_CUT:Z_ROWS, :])
+        resT = keep.tile([P, P], F32, align_bytes=64)
+        nc.vector.transpose(out=resT[:], in_=res[:])
+        out_blocks = out.rearrange("i r (j n) -> (i r j) n", j=N_TILES).rearrange(
+            "(F f) (Q q) -> Q f F q", f=BLOCK, q=BLOCK
+        )
+        for quadrant in range(P // BLOCK):
+            queue = nc.sync if quadrant < 2 else nc.scalar
+            queue.dma_start(
+                out=out_blocks[quadrant],
+                in_=resT[quadrant * BLOCK : (quadrant + 1) * BLOCK, 0:Z_ROWS].rearrange(
+                    "f (F q) -> f F q", q=BLOCK
+                ),
+            )

@@ -28,17 +28,9 @@ N_TILES = B // P
 Z_ROWS = ORD * R * N_TILES
 BLOCK = 32
 HALF = 256
-RUN = 1
-LAG = 1
+WARM = 4
 
 FLOPS = 2 * Q * KRON * B + 2 * 2 * KRON * B + 3 * 2 * RR * B
-
-
-def regroup(copy, grouped, raw):
-    copy(
-        out=grouped.rearrange("p (w i) t -> p w t i", i=RUN),
-        in_=raw.rearrange("p t (w i) -> p w t i", i=RUN),
-    )
 
 
 def tile_fast_tucker_taylor_pa_s_kernel(tc, z, G2, grad_out, out):
@@ -60,32 +52,52 @@ def tile_fast_tucker_taylor_pa_s_kernel(tc, z, G2, grad_out, out):
         res = keep.tile([P, P], F32, align_bytes=64)
         nc.vector.memset(res[:], 0.0)
 
-        raw_w = []
-        raw_g = []
+        raw = {}
         for c in range(PASSES):
-            for source, raws, label in ((G2, raw_w, "w"), (grad_out, raw_g, "g")):
-                raw = keep.tile([P, PACK, 2 * HALF], BF16, name="raw_%s%d" % (label, c))
+            for source, label in ((G2, "w"), (grad_out, "g")):
+                loaded = keep.tile([P, PACK, 2 * HALF], BF16, name="raw_%s%d" % (label, c))
                 nc.sync.dma_start(
-                    out=raw[:],
+                    out=loaded[:],
                     in_=source[c * K_PASS : (c + 1) * K_PASS, :].rearrange(
                         "(p t) w -> p t w", t=PACK
                     ),
                 )
-                raws.append(raw)
+                raw[(label, c)] = loaded
 
-        grouped_w = keep.tile([P, PASSES, KRON, PACK], BF16, align_bytes=64)
-        w_codes = keep.tile([P, PASSES, KRON], U32, align_bytes=64)
-        w_scales = keep.tile([P, PASSES, KRON], U8, align_bytes=64)
-        grouped_g = keep.tile([P, 2, PASSES, HALF, PACK], BF16, align_bytes=64)
-        g_codes = keep.tile([P, 2, PASSES, HALF], U32, align_bytes=64)
-        g_scales = keep.tile([P, 2, PASSES, HALF], U8, align_bytes=64)
+        warm_bf_ps = psum.tile([P, P], BF16)
+        nc.tensor.transpose(warm_bf_ps[:], raw[("w", 0)][:, 0, 0:P], ident_bf[:])
+        warm_ps = psum.tile([P, P], F32)
+        for i in range(WARM):
+            nc.tensor.matmul(
+                out=warm_ps[:], lhsT=ident_f32[:], rhs=ident_f32[:], start=True, stop=True
+            )
 
-        def quantise_w(c, half):
-            columns = slice(half * HALF, (half + 1) * HALF)
+        grouped = {}
+        codes = {}
+        scales = {}
+        for label in ("w", "g"):
+            grouped[label] = keep.tile(
+                [P, PASSES, 2 * HALF, PACK], BF16, align_bytes=64, name="grouped_%s" % label
+            )
+            codes[label] = keep.tile(
+                [P, PASSES, 2 * HALF], U32, align_bytes=64, name="codes_%s" % label
+            )
+            scales[label] = keep.tile(
+                [P, PASSES, 2 * HALF], U8, align_bytes=64, name="scales_%s" % label
+            )
+        formats = {"w": E4M3X4, "g": E5M2X4}
+
+        def regroup(copy, label, c, first, last):
+            copy(
+                out=grouped[label][:, c, first:last, :],
+                in_=raw[(label, c)][:, :, first:last].rearrange("p t w -> p w t"),
+            )
+
+        def quantise(label, c, first, last):
             nc.vector.quantize_mx(
-                out=w_codes[:, c, columns].bitcast(E4M3X4),
-                scales=w_scales[:, c, columns],
-                in_=grouped_w[:, c, columns, :].rearrange("p w t -> p (w t)"),
+                out=codes[label][:, c, first:last].bitcast(formats[label]),
+                scales=scales[label][:, c, first:last],
+                in_=grouped[label][:, c, first:last, :].rearrange("p w t -> p (w t)"),
             )
 
         dT = []
@@ -93,76 +105,63 @@ def tile_fast_tucker_taylor_pa_s_kernel(tc, z, G2, grad_out, out):
             dT.append(psum.tile([P, KRON], F32, name="dT%d" % j))
 
         def mx_pass(j, c):
-            half = j // 2
-            samples = slice((j % 2) * P, (j % 2 + 1) * P)
+            samples = slice(j * P, (j + 1) * P)
             nc.tensor.matmul_mx(
                 out=dT[j][:],
-                lhsT=g_codes[:, half, c, samples].bitcast(E5M2X4),
-                lhsT_scale=g_scales[:, half, c, samples],
-                rhs=w_codes[:, c, :].bitcast(E4M3X4),
-                rhs_scale=w_scales[:, c, :],
+                lhsT=codes["g"][:, c, samples].bitcast(E5M2X4),
+                lhsT_scale=scales["g"][:, c, samples],
+                rhs=codes["w"][:, c, :].bitcast(E4M3X4),
+                rhs_scale=scales["w"][:, c, :],
                 start=(c == 0),
                 stop=(c == PASSES - 1),
             )
 
-        def regroup_w(c):
-            regroup(nc.vector.tensor_copy, grouped_w[:, c, 0:HALF, :], raw_w[c][:, :, 0:HALF])
-            regroup(nc.scalar.copy, grouped_w[:, c, HALF:, :], raw_w[c][:, :, HALF:])
-
-        def regroup_g(c):
-            regroup(nc.vector.tensor_copy, grouped_g[:, 0, c, :, :], raw_g[c][:, :, 0:HALF])
-            regroup(nc.scalar.copy, grouped_g[:, 1, c, :, :], raw_g[c][:, :, HALF:])
-
-        def multiply_half(half, c):
-            nc.vector.quantize_mx(
-                out=g_codes[:, half, c, :].bitcast(E5M2X4),
-                scales=g_scales[:, half, c, :],
-                in_=grouped_g[:, half, c, :, :].rearrange("p w t -> p (w t)"),
-            )
-            mx_pass(2 * half, c)
-            mx_pass(2 * half + 1, c)
-
-        regroup_w(0)
-        quantise_w(0, 0)
-        regroup_g(0)
-        quantise_w(0, 1)
-        multiply_half(0, 0)
-        regroup_w(1)
-        multiply_half(1, 0)
-        quantise_w(1, 0)
-        regroup_g(1)
+        vector_copy = nc.vector.tensor_copy
+        scalar_copy = nc.scalar.copy
+        regroup(vector_copy, "w", 0, 0, HALF)
+        regroup(vector_copy, "w", 0, HALF, HALF + P)
+        regroup(scalar_copy, "w", 0, HALF + P, 2 * HALF)
+        quantise("w", 0, 0, HALF)
+        regroup(vector_copy, "g", 0, 0, HALF)
+        regroup(scalar_copy, "g", 0, HALF, 2 * HALF)
+        quantise("w", 0, HALF, 2 * HALF)
+        quantise("g", 0, 0, HALF)
+        mx_pass(0, 0)
+        mx_pass(1, 0)
+        regroup(vector_copy, "w", 1, 0, HALF)
+        regroup(scalar_copy, "w", 1, HALF, 2 * HALF)
+        quantise("g", 0, HALF, 2 * HALF)
+        mx_pass(2, 0)
+        mx_pass(3, 0)
+        quantise("w", 1, 0, HALF)
         zT_ps = psum.tile([P, P], BF16)
         nc.tensor.transpose(zT_ps[:], z_rows[:], ident_bf[:])
+        regroup(vector_copy, "g", 1, 0, HALF)
+        regroup(scalar_copy, "g", 1, HALF, HALF + P)
+        regroup(scalar_copy, "g", 1, HALF + P, 2 * HALF)
+        quantise("w", 1, HALF, 2 * HALF)
+        for j in range(N_TILES):
+            quantise("g", 1, j * P, (j + 1) * P)
+            mx_pass(j, 1)
         zT = keep.tile([P, ORD, N_TILES, R], F32)
-        nc.scalar.copy(
+        nc.vector.tensor_copy(
             out=zT[:], in_=zT_ps[:, 0:Z_ROWS].rearrange("p (i r j) -> p i j r", i=ORD, r=R)
         )
-        quantise_w(1, 1)
-        multiply_half(0, 1)
-        multiply_half(1, 1)
 
         tu = keep.tile([P, 2, N_TILES, RR], F32)
 
-        def contract_step(acc, d_slice, z_column, first):
-            if first:
-                nc.vector.tensor_scalar_mul(out=acc, in0=d_slice, scalar1=z_column)
-            else:
-                nc.vector.scalar_tensor_tensor(
-                    out=acc, in0=d_slice, scalar=z_column, in1=acc, op0=MULT, op1=ADD
-                )
-
-        def d_slices(j, s):
-            return (
-                (dT[j][:, s * RR : (s + 1) * RR], zT[:, 2, j, s : s + 1]),
-                (dT[j][:].rearrange("p (cb a) -> p cb a", a=R)[:, :, s], zT[:, 0, j, s : s + 1]),
-            )
+        def d_slice(j, s, k):
+            if k == 0:
+                return dT[j][:, s * RR : (s + 1) * RR], zT[:, 2, j, s : s + 1]
+            return dT[j][:].rearrange("p (cb a) -> p cb a", a=R)[:, :, s], zT[:, 0, j, s : s + 1]
 
         last = N_TILES - 1
         terms = keep.tile([P, R, 2, RR], F32)
         tu_last_ps = psum.tile([P, 2, RR], F32)
         for s in range(R):
-            for k, (d_slice, z_column) in enumerate(d_slices(last, s)):
-                nc.scalar.activation(out=terms[:, s, k, :], in_=d_slice, func=COPY, scale=z_column)
+            for k in range(2):
+                d_term, z_column = d_slice(last, s, k)
+                nc.scalar.activation(out=terms[:, s, k, :], in_=d_term, func=COPY, scale=z_column)
             nc.tensor.matmul(
                 out=tu_last_ps[:].rearrange("p k x -> p (k x)"),
                 lhsT=ident_f32[:],
@@ -172,12 +171,23 @@ def tile_fast_tucker_taylor_pa_s_kernel(tc, z, G2, grad_out, out):
             )
         nc.scalar.copy(out=tu[:, :, last, :], in_=tu_last_ps[:])
 
-        for turn in range(R + LAG):
-            for j in range(last):
-                s = turn - LAG if j == 2 else turn
-                if 0 <= s < R:
-                    for k, (d_slice, z_column) in enumerate(d_slices(j, s)):
-                        contract_step(tu[:, k, j, :], d_slice, z_column, s == 0)
+        for s in range(R):
+            for k in range(2):
+                for j in range(last):
+                    d_term, z_column = d_slice(j, s, k)
+                    if s == 0:
+                        nc.vector.tensor_scalar_mul(
+                            out=tu[:, k, j, :], in0=d_term, scalar1=z_column
+                        )
+                    else:
+                        nc.vector.scalar_tensor_tensor(
+                            out=tu[:, k, j, :],
+                            in0=d_term,
+                            scalar=z_column,
+                            in1=tu[:, k, j, :],
+                            op0=MULT,
+                            op1=ADD,
+                        )
 
         prod0 = keep.tile([P, N_TILES, R, R], F32)
         nc.vector.tensor_tensor(

@@ -28,6 +28,7 @@ N_TILES = B // P
 Z_ROWS = ORD * R * N_TILES
 BLOCK = 32
 HALF = 256
+TILE_ORDER = (0, 2, 1, 3)
 WARM = 4
 
 FLOPS = 2 * Q * KRON * B + 2 * 2 * KRON * B + 3 * 2 * RR * B
@@ -49,8 +50,7 @@ def tile_fast_tucker_taylor_pa_s_kernel(tc, z, G2, grad_out, out):
         make_identity(nc, ident_bf[:])
         ident_f32 = keep.tile([P, P], F32)
         make_identity(nc, ident_f32[:])
-        res = keep.tile([P, P], F32, align_bytes=64)
-        nc.vector.memset(res[:], 0.0)
+        res = keep.tile([P, Z_ROWS], F32, align_bytes=64)
 
         raw = {}
         for c in range(PASSES):
@@ -130,23 +130,24 @@ def tile_fast_tucker_taylor_pa_s_kernel(tc, z, G2, grad_out, out):
         mx_pass(1, 0)
         regroup(vector_copy, "w", 1, 0, HALF)
         regroup(scalar_copy, "w", 1, HALF, 2 * HALF)
+        zT_ps = psum.tile([P, P], BF16)
+        nc.tensor.transpose(zT_ps[:], z_rows[:], ident_bf[:])
         quantise("g", 0, HALF, 2 * HALF)
         mx_pass(2, 0)
         mx_pass(3, 0)
         quantise("w", 1, 0, HALF)
-        zT_ps = psum.tile([P, P], BF16)
-        nc.tensor.transpose(zT_ps[:], z_rows[:], ident_bf[:])
-        regroup(vector_copy, "g", 1, 0, HALF)
-        regroup(scalar_copy, "g", 1, HALF, HALF + P)
-        regroup(scalar_copy, "g", 1, HALF + P, 2 * HALF)
         quantise("w", 1, HALF, 2 * HALF)
-        for j in range(N_TILES):
-            quantise("g", 1, j * P, (j + 1) * P)
-            mx_pass(j, 1)
         zT = keep.tile([P, ORD, N_TILES, R], F32)
         nc.vector.tensor_copy(
             out=zT[:], in_=zT_ps[:, 0:Z_ROWS].rearrange("p (i r j) -> p i j r", i=ORD, r=R)
         )
+        regroup(vector_copy, "g", 1, 0, P)
+        regroup(vector_copy, "g", 1, P, HALF)
+        regroup(scalar_copy, "g", 1, HALF, HALF + P)
+        regroup(scalar_copy, "g", 1, HALF + P, 2 * HALF)
+        for j in TILE_ORDER:
+            quantise("g", 1, j * P, (j + 1) * P)
+            mx_pass(j, 1)
 
         tu = keep.tile([P, 2, N_TILES, RR], F32)
 
@@ -169,11 +170,10 @@ def tile_fast_tucker_taylor_pa_s_kernel(tc, z, G2, grad_out, out):
                 start=(s == 0),
                 stop=(s == R - 1),
             )
-        nc.scalar.copy(out=tu[:, :, last, :], in_=tu_last_ps[:])
 
         for s in range(R):
             for k in range(2):
-                for j in range(last):
+                for j in TILE_ORDER[0:last]:
                     d_term, z_column = d_slice(j, s, k)
                     if s == 0:
                         nc.vector.tensor_scalar_mul(
@@ -189,39 +189,40 @@ def tile_fast_tucker_taylor_pa_s_kernel(tc, z, G2, grad_out, out):
                             op1=ADD,
                         )
 
-        prod0 = keep.tile([P, N_TILES, R, R], F32)
-        nc.vector.tensor_tensor(
-            out=prod0[:],
-            in0=tu[:, 0, :, :].rearrange("p j (b a) -> p j b a", a=R),
-            in1=zT[:, 1, :, :].unsqueeze(3).to_broadcast([P, N_TILES, R, R]),
-            op=MULT,
-        )
-        prod12 = keep.tile([P, 2 * N_TILES, R, R], F32)
-        nc.vector.tensor_tensor(
-            out=prod12[:],
-            in0=tu[:].rearrange("p s j (x y) -> p (s j) x y", y=R),
-            in1=zT[:, 0:2, :, :]
-            .rearrange("p i j r -> p (i j) r")
-            .unsqueeze(2)
-            .to_broadcast([P, 2 * N_TILES, R, R]),
-            op=MULT,
-        )
-        res_view = res[:, 0:Z_ROWS].rearrange("p (i r j) -> p i j r", i=ORD, r=R)
-        nc.vector.tensor_reduce(
-            out=res_view[:, 0, :, :],
-            in_=prod0[:].rearrange("p j b a -> p j a b"),
-            axis=AXIS_X,
-            op=ADD,
-        )
-        nc.vector.tensor_reduce(
-            out=res_view[:, 1:3, :, :],
-            in_=prod12[:].rearrange("p (s j) x y -> p s j x y", s=2),
-            axis=AXIS_X,
-            op=ADD,
-        )
+        prod = keep.tile([P, ORD, N_TILES, R, R], F32)
 
-        resT = keep.tile([P, P], F32, align_bytes=64)
-        nc.vector.transpose(out=resT[:], in_=res[:])
+        def multiply(i, tiles, sums):
+            count = tiles.stop - tiles.start
+            if i == 0:
+                factor = zT[:, 1, tiles, :].unsqueeze(3).to_broadcast([P, count, R, R])
+            else:
+                factor = zT[:, i - 1, tiles, :].unsqueeze(2).to_broadcast([P, count, R, R])
+            nc.vector.tensor_tensor(
+                out=prod[:, i, tiles, :, :],
+                in0=sums.rearrange("p j (x y) -> p j x y", y=R),
+                in1=factor,
+                op=MULT,
+            )
+
+        mine = slice(0, last)
+        other = slice(last, N_TILES)
+        multiply(0, mine, tu[:, 0, mine, :])
+        multiply(1, mine, tu[:, 0, mine, :])
+        multiply(0, other, tu_last_ps[:, 0:1, :])
+        multiply(1, other, tu_last_ps[:, 0:1, :])
+        multiply(2, mine, tu[:, 1, mine, :])
+        multiply(2, other, tu_last_ps[:, 1:2, :])
+        res_view = res[:].rearrange("p (i r j) -> p i j r", i=ORD, r=R)
+        for i in range(ORD):
+            products = prod[:, i, :, :, :]
+            if i == 0:
+                products = products.rearrange("p j b a -> p j a b")
+            nc.vector.tensor_reduce(out=res_view[:, i, :, :], in_=products, axis=AXIS_X, op=ADD)
+
+        resT = keep.tile([P, Z_ROWS], F32, align_bytes=64)
+        for i in range(ORD):
+            block = slice(i * BLOCK, (i + 1) * BLOCK)
+            nc.vector.transpose(out=resT[:, block], in_=res[:, block])
         out_blocks = out.rearrange("i r (j n) -> (i r j) n", j=N_TILES).rearrange(
             "(F f) (Q q) -> Q f F q", f=BLOCK, q=BLOCK
         )
@@ -229,7 +230,7 @@ def tile_fast_tucker_taylor_pa_s_kernel(tc, z, G2, grad_out, out):
             queue = nc.sync if quadrant < 2 else nc.scalar
             queue.dma_start(
                 out=out_blocks[quadrant],
-                in_=resT[quadrant * BLOCK : (quadrant + 1) * BLOCK, 0:Z_ROWS].rearrange(
+                in_=resT[quadrant * BLOCK : (quadrant + 1) * BLOCK, :].rearrange(
                     "f (F q) -> f F q", q=BLOCK
                 ),
             )

@@ -29,6 +29,7 @@ Z_ROWS = ORD * R * N_TILES
 BLOCK = 32
 HALF = 256
 TILE_ORDER = (0, 2, 1, 3)
+OUTPUT_ORDER = (2, 0, 1)
 WARM = 4
 
 FLOPS = 2 * Q * KRON * B + 2 * 2 * KRON * B + 3 * 2 * RR * B
@@ -64,12 +65,15 @@ def tile_fast_tucker_taylor_pa_s_kernel(tc, z, G2, grad_out, out):
                 )
                 raw[(label, c)] = loaded
 
-        warm_bf_ps = psum.tile([P, P], BF16)
-        nc.tensor.transpose(warm_bf_ps[:], raw[("w", 0)][:, 0, 0:P], ident_bf[:])
-        warm_ps = psum.tile([P, P], F32)
+        small_bf_ps = psum.tile([P, 2, P], BF16)
+        small_ps = psum.tile([P, 3, P], F32)
+        turned_ps = psum.tile([P, 2, P], F32)
+        terms = keep.tile([P, 2, R, 2, RR], F32)
+        nc.vector.memset(terms[:, 0, :, 0, :], 0.0)
+        nc.tensor.transpose(small_bf_ps[:, 0, :], raw[("w", 0)][:, 0, 0:P], ident_bf[:])
         for i in range(WARM):
             nc.tensor.matmul(
-                out=warm_ps[:], lhsT=ident_f32[:], rhs=ident_f32[:], start=True, stop=True
+                out=small_ps[:, 0, :], lhsT=ident_f32[:], rhs=ident_f32[:], start=True, stop=True
             )
 
         grouped = {}
@@ -130,8 +134,8 @@ def tile_fast_tucker_taylor_pa_s_kernel(tc, z, G2, grad_out, out):
         mx_pass(1, 0)
         regroup(vector_copy, "w", 1, 0, HALF)
         regroup(scalar_copy, "w", 1, HALF, 2 * HALF)
-        zT_ps = psum.tile([P, P], BF16)
-        nc.tensor.transpose(zT_ps[:], z_rows[:], ident_bf[:])
+        zT_ps = small_bf_ps[:, 1, :]
+        nc.tensor.transpose(zT_ps, z_rows[:], ident_bf[:])
         quantise("g", 0, HALF, 2 * HALF)
         mx_pass(2, 0)
         mx_pass(3, 0)
@@ -156,38 +160,53 @@ def tile_fast_tucker_taylor_pa_s_kernel(tc, z, G2, grad_out, out):
                 return dT[j][:, s * RR : (s + 1) * RR], zT[:, 2, j, s : s + 1]
             return dT[j][:].rearrange("p (cb a) -> p cb a", a=R)[:, :, s], zT[:, 0, j, s : s + 1]
 
-        last = N_TILES - 1
-        terms = keep.tile([P, R, 2, RR], F32)
-        tu_last_ps = psum.tile([P, 2, RR], F32)
-        for s in range(R):
-            for k in range(2):
-                d_term, z_column = d_slice(last, s, k)
-                nc.scalar.activation(out=terms[:, s, k, :], in_=d_term, func=COPY, scale=z_column)
-            nc.tensor.matmul(
-                out=tu_last_ps[:].rearrange("p k x -> p (k x)"),
-                lhsT=ident_f32[:],
-                rhs=terms[:, s, :, :].rearrange("p k x -> p (k x)"),
-                start=(s == 0),
-                stop=(s == R - 1),
-            )
-
-        for s in range(R):
-            for k in range(2):
-                for j in TILE_ORDER[0:last]:
+        first = TILE_ORDER[0]
+        last = TILE_ORDER[N_TILES - 1]
+        shares = ((first, (1,)), (last, (0, 1)))
+        for slot, (j, kinds) in enumerate(shares):
+            for s in range(R):
+                for k in kinds:
                     d_term, z_column = d_slice(j, s, k)
-                    if s == 0:
-                        nc.vector.tensor_scalar_mul(
-                            out=tu[:, k, j, :], in0=d_term, scalar1=z_column
-                        )
-                    else:
-                        nc.vector.scalar_tensor_tensor(
-                            out=tu[:, k, j, :],
-                            in0=d_term,
-                            scalar=z_column,
-                            in1=tu[:, k, j, :],
-                            op0=MULT,
-                            op1=ADD,
-                        )
+                    nc.scalar.activation(
+                        out=terms[:, slot, s, k, :], in_=d_term, func=COPY, scale=z_column
+                    )
+                nc.tensor.matmul(
+                    out=turned_ps[:, slot, :],
+                    lhsT=terms[:, slot, s, :, :].rearrange("p k x -> p (k x)"),
+                    rhs=ident_f32[:],
+                    is_transpose=True,
+                    start=(s == 0),
+                    stop=(s == R - 1),
+                )
+        turned = keep.tile([P, 2, P], F32)
+        nc.scalar.copy(out=turned[:], in_=turned_ps[:])
+        for slot in range(2):
+            nc.tensor.transpose(small_ps[:, 1 + slot, :], turned[:, slot, :], ident_f32[:])
+        tu_first_ps = small_ps[:, 1, :].rearrange("p (k x) -> p k x", k=2)
+        tu_last_ps = small_ps[:, 2, :].rearrange("p (k x) -> p k x", k=2)
+
+        def vector_step(j, s, k):
+            if not 0 <= s < R:
+                return
+            d_term, z_column = d_slice(j, s, k)
+            if s == 0:
+                nc.vector.tensor_scalar_mul(out=tu[:, k, j, :], in0=d_term, scalar1=z_column)
+            else:
+                nc.vector.scalar_tensor_tensor(
+                    out=tu[:, k, j, :],
+                    in0=d_term,
+                    scalar=z_column,
+                    in1=tu[:, k, j, :],
+                    op0=MULT,
+                    op1=ADD,
+                )
+
+        middle = TILE_ORDER[1 : N_TILES - 1]
+        for turn in range(R + 1):
+            vector_step(first, turn - 1, 0)
+            for k in range(2):
+                for j in middle:
+                    vector_step(j, turn, k)
 
         prod = keep.tile([P, ORD, N_TILES, R, R], F32)
 
@@ -204,23 +223,22 @@ def tile_fast_tucker_taylor_pa_s_kernel(tc, z, G2, grad_out, out):
                 op=MULT,
             )
 
-        mine = slice(0, last)
-        other = slice(last, N_TILES)
-        multiply(0, mine, tu[:, 0, mine, :])
-        multiply(1, mine, tu[:, 0, mine, :])
-        multiply(0, other, tu_last_ps[:, 0:1, :])
-        multiply(1, other, tu_last_ps[:, 0:1, :])
-        multiply(2, mine, tu[:, 1, mine, :])
-        multiply(2, other, tu_last_ps[:, 1:2, :])
+        multiply(2, slice(first, first + 1), tu_first_ps[:, 1:2, :])
+        multiply(2, slice(last, last + 1), tu_last_ps[:, 1:2, :])
+        multiply(0, slice(last, last + 1), tu_last_ps[:, 0:1, :])
+        multiply(1, slice(last, last + 1), tu_last_ps[:, 0:1, :])
+        multiply(2, slice(1, last), tu[:, 1, 1:last, :])
+        multiply(0, slice(0, last), tu[:, 0, 0:last, :])
+        multiply(1, slice(0, last), tu[:, 0, 0:last, :])
         res_view = res[:].rearrange("p (i r j) -> p i j r", i=ORD, r=R)
-        for i in range(ORD):
+        for i in OUTPUT_ORDER:
             products = prod[:, i, :, :, :]
             if i == 0:
                 products = products.rearrange("p j b a -> p j a b")
             nc.vector.tensor_reduce(out=res_view[:, i, :, :], in_=products, axis=AXIS_X, op=ADD)
 
         resT = keep.tile([P, Z_ROWS], F32, align_bytes=64)
-        for i in range(ORD):
+        for i in OUTPUT_ORDER:
             block = slice(i * BLOCK, (i + 1) * BLOCK)
             nc.vector.transpose(out=resT[:, block], in_=res[:, block])
         out_blocks = out.rearrange("i r (j n) -> (i r j) n", j=N_TILES).rearrange(

@@ -28,7 +28,7 @@ N_TILES = B // P
 Z_ROWS = ORD * R * N_TILES
 BLOCK = 32
 HALF = 256
-TILE_ORDER = (0, 2, 1, 3)
+TILE_ORDER = (0, 1, 2, 3)
 OUTPUT_ORDER = (2, 0, 1)
 WARM = 4
 
@@ -145,9 +145,9 @@ def tile_fast_tucker_taylor_pa_s_kernel(tc, z, G2, grad_out, out):
         nc.vector.tensor_copy(
             out=zT[:], in_=zT_ps[:, 0:Z_ROWS].rearrange("p (i r j) -> p i j r", i=ORD, r=R)
         )
-        regroup(vector_copy, "g", 1, 0, P)
         regroup(vector_copy, "g", 1, P, HALF)
-        regroup(scalar_copy, "g", 1, HALF, HALF + P)
+        regroup(vector_copy, "g", 1, HALF, HALF + P)
+        regroup(scalar_copy, "g", 1, 0, P)
         regroup(scalar_copy, "g", 1, HALF + P, 2 * HALF)
         for j in TILE_ORDER:
             quantise("g", 1, j * P, (j + 1) * P)

@@ -28,8 +28,10 @@ N_TILES = B // P
 Z_ROWS = ORD * R * N_TILES
 BLOCK = 32
 HALF = 256
-TILE_ORDER = (0, 1, 2, 3)
-OUTPUT_ORDER = (2, 0, 1)
+TILE_ORDER = (0, 3, 1, 2)
+SHARED, SCALAR = 0, 3
+VECTOR = (1, 2)
+OUTPUT_ORDER = (0, 2, 1)
 WARM = 4
 
 FLOPS = 2 * Q * KRON * B + 2 * 2 * KRON * B + 3 * 2 * RR * B
@@ -43,10 +45,10 @@ def tile_fast_tucker_taylor_pa_s_kernel(tc, z, G2, grad_out, out):
         ctx.enter_context(tc.manual_schedule())
 
         z_rows = keep.tile([P, P], BF16)
-        nc.vector.memset(z_rows[:], 0.0)
-        nc.scalar.dma_start(
-            out=z_rows[0:Z_ROWS, :], in_=z.rearrange("i r (j n) -> (i r j) n", j=N_TILES)
-        )
+        z_view = z.rearrange("i r (j n) -> (i r j) n", j=N_TILES)
+        nc.scalar.dma_start(out=z_rows[0:64, :], in_=z_view[0:64, :])
+        nc.scalar.dma_start(out=z_rows[64:Z_ROWS, :], in_=z_view[64:Z_ROWS, :])
+        nc.vector.memset(z_rows[Z_ROWS:P, :], 0.0)
         ident_bf = keep.tile([P, P], BF16)
         make_identity(nc, ident_bf[:])
         ident_f32 = keep.tile([P, P], F32)
@@ -69,12 +71,14 @@ def tile_fast_tucker_taylor_pa_s_kernel(tc, z, G2, grad_out, out):
         small_ps = psum.tile([P, 3, P], F32)
         turned_ps = psum.tile([P, 2, P], F32)
         terms = keep.tile([P, 2, R, 2, RR], F32)
-        nc.vector.memset(terms[:, 0, :, 0, :], 0.0)
         nc.tensor.transpose(small_bf_ps[:, 0, :], raw[("w", 0)][:, 0, 0:P], ident_bf[:])
+        zT_ps = small_bf_ps[:, 1, :]
         for i in range(WARM):
             nc.tensor.matmul(
                 out=small_ps[:, 0, :], lhsT=ident_f32[:], rhs=ident_f32[:], start=True, stop=True
             )
+            if i == 1:
+                nc.tensor.transpose(zT_ps, z_rows[:], ident_bf[:])
 
         grouped = {}
         codes = {}
@@ -134,17 +138,15 @@ def tile_fast_tucker_taylor_pa_s_kernel(tc, z, G2, grad_out, out):
         mx_pass(1, 0)
         regroup(vector_copy, "w", 1, 0, HALF)
         regroup(scalar_copy, "w", 1, HALF, 2 * HALF)
-        zT_ps = small_bf_ps[:, 1, :]
-        nc.tensor.transpose(zT_ps, z_rows[:], ident_bf[:])
+        zT = keep.tile([P, ORD, N_TILES, R], F32)
+        nc.scalar.copy(
+            out=zT[:], in_=zT_ps[:, 0:Z_ROWS].rearrange("p (i r j) -> p i j r", i=ORD, r=R)
+        )
         quantise("g", 0, HALF, 2 * HALF)
         mx_pass(2, 0)
         mx_pass(3, 0)
         quantise("w", 1, 0, HALF)
         quantise("w", 1, HALF, 2 * HALF)
-        zT = keep.tile([P, ORD, N_TILES, R], F32)
-        nc.vector.tensor_copy(
-            out=zT[:], in_=zT_ps[:, 0:Z_ROWS].rearrange("p (i r j) -> p i j r", i=ORD, r=R)
-        )
         regroup(vector_copy, "g", 1, P, HALF)
         regroup(vector_copy, "g", 1, HALF, HALF + P)
         regroup(scalar_copy, "g", 1, 0, P)
@@ -153,22 +155,28 @@ def tile_fast_tucker_taylor_pa_s_kernel(tc, z, G2, grad_out, out):
             quantise("g", 1, j * P, (j + 1) * P)
             mx_pass(j, 1)
 
-        tu = keep.tile([P, 2, N_TILES, RR], F32)
-
         def d_slice(j, s, k):
             if k == 0:
-                return dT[j][:, s * RR : (s + 1) * RR], zT[:, 2, j, s : s + 1]
-            return dT[j][:].rearrange("p (cb a) -> p cb a", a=R)[:, :, s], zT[:, 0, j, s : s + 1]
+                d_term = dT[j][:, s * RR : (s + 1) * RR].rearrange("p (b a) -> p a b", a=R)
+                return d_term, zT[:, 2, j, s : s + 1]
+            d_term = dT[j][:].rearrange("p (c b a) -> p c b a", b=R, a=R)[:, :, :, s]
+            return d_term, zT[:, 0, j, s : s + 1]
 
-        first = TILE_ORDER[0]
-        last = TILE_ORDER[N_TILES - 1]
-        shares = ((first, (1,)), (last, (0, 1)))
-        for slot, (j, kinds) in enumerate(shares):
+        nc.vector.tensor_tensor(
+            out=terms[:, 0, :, 0, :].rearrange("p c (a b) -> p c a b", b=R),
+            in0=dT[SHARED][:].rearrange("p (c b a) -> p c a b", b=R, a=R),
+            in1=zT[:, 2, SHARED, :].unsqueeze(2).unsqueeze(3).to_broadcast([P, R, R, R]),
+            op=MULT,
+        )
+        for slot, j, kinds in ((1, SCALAR, (0, 1)), (0, SHARED, (1,))):
             for s in range(R):
                 for k in kinds:
                     d_term, z_column = d_slice(j, s, k)
                     nc.scalar.activation(
-                        out=terms[:, slot, s, k, :], in_=d_term, func=COPY, scale=z_column
+                        out=terms[:, slot, s, k, :].rearrange("p (y b) -> p y b", b=R),
+                        in_=d_term,
+                        func=COPY,
+                        scale=z_column,
                     )
                 nc.tensor.matmul(
                     out=turned_ps[:, slot, :],
@@ -182,60 +190,56 @@ def tile_fast_tucker_taylor_pa_s_kernel(tc, z, G2, grad_out, out):
         nc.scalar.copy(out=turned[:], in_=turned_ps[:])
         for slot in range(2):
             nc.tensor.transpose(small_ps[:, 1 + slot, :], turned[:, slot, :], ident_f32[:])
-        tu_first_ps = small_ps[:, 1, :].rearrange("p (k x) -> p k x", k=2)
-        tu_last_ps = small_ps[:, 2, :].rearrange("p (k x) -> p k x", k=2)
 
-        def vector_step(j, s, k):
-            if not 0 <= s < R:
-                return
+        tu = keep.tile([P, 2, 2, RR], F32)
+
+        def vector_step(slot, j, s, k):
             d_term, z_column = d_slice(j, s, k)
+            total = tu[:, slot, k, :].rearrange("p (y b) -> p y b", b=R)
             if s == 0:
-                nc.vector.tensor_scalar_mul(out=tu[:, k, j, :], in0=d_term, scalar1=z_column)
+                nc.vector.tensor_scalar_mul(out=total, in0=d_term, scalar1=z_column)
             else:
                 nc.vector.scalar_tensor_tensor(
-                    out=tu[:, k, j, :],
-                    in0=d_term,
-                    scalar=z_column,
-                    in1=tu[:, k, j, :],
-                    op0=MULT,
-                    op1=ADD,
+                    out=total, in0=d_term, scalar=z_column, in1=total, op0=MULT, op1=ADD
                 )
 
-        middle = TILE_ORDER[1 : N_TILES - 1]
-        for turn in range(R + 1):
-            vector_step(first, turn - 1, 0)
+        for s in range(R):
             for k in range(2):
-                for j in middle:
-                    vector_step(j, turn, k)
+                for slot, j in enumerate(VECTOR):
+                    vector_step(slot, j, s, k)
 
-        prod = keep.tile([P, ORD, N_TILES, R, R], F32)
+        prod_b = keep.tile([P, 2 * R, N_TILES, R], F32)
+        prod_a = keep.tile([P, R, N_TILES, R], F32)
 
-        def multiply(i, tiles, sums):
-            count = tiles.stop - tiles.start
-            if i == 0:
-                factor = zT[:, 1, tiles, :].unsqueeze(3).to_broadcast([P, count, R, R])
-            else:
-                factor = zT[:, i - 1, tiles, :].unsqueeze(2).to_broadcast([P, count, R, R])
+        def multiply(tiles, sums):
             nc.vector.tensor_tensor(
-                out=prod[:, i, tiles, :, :],
-                in0=sums.rearrange("p j (x y) -> p j x y", y=R),
-                in1=factor,
+                out=prod_b[:, :, tiles, :],
+                in0=sums.rearrange("p j (y b) -> p y j b", b=R),
+                in1=zT[:, 1, tiles, :].unsqueeze(1).to_broadcast([P, 2 * R, 2, R]),
+                op=MULT,
+            )
+            nc.vector.tensor_tensor(
+                out=prod_a[:, :, tiles, :],
+                in0=sums[:, :, 0:RR].rearrange("p j (a b) -> p b j a", b=R),
+                in1=zT[:, 0, tiles, :].unsqueeze(1).to_broadcast([P, R, 2, R]),
                 op=MULT,
             )
 
-        multiply(2, slice(first, first + 1), tu_first_ps[:, 1:2, :])
-        multiply(2, slice(last, last + 1), tu_last_ps[:, 1:2, :])
-        multiply(0, slice(last, last + 1), tu_last_ps[:, 0:1, :])
-        multiply(1, slice(last, last + 1), tu_last_ps[:, 0:1, :])
-        multiply(2, slice(1, last), tu[:, 1, 1:last, :])
-        multiply(0, slice(0, last), tu[:, 0, 0:last, :])
-        multiply(1, slice(0, last), tu[:, 0, 0:last, :])
-        res_view = res[:].rearrange("p (i r j) -> p i j r", i=ORD, r=R)
-        for i in OUTPUT_ORDER:
-            products = prod[:, i, :, :, :]
-            if i == 0:
-                products = products.rearrange("p j b a -> p j a b")
-            nc.vector.tensor_reduce(out=res_view[:, i, :, :], in_=products, axis=AXIS_X, op=ADD)
+        multiply(slice(1, SCALAR), tu[:].rearrange("p j k x -> p j (k x)"))
+        multiply(slice(SHARED, N_TILES, SCALAR), small_ps[:, 1:3, :])
+        res_view = res[:].rearrange("p (i x) -> p i x", i=ORD)
+        nc.vector.tensor_reduce(
+            out=res_view[:, 0:ORD:2, :],
+            in_=prod_b[:].rearrange("p (k r) j b -> p k (r j) b", k=2),
+            axis=AXIS_X,
+            op=ADD,
+        )
+        nc.vector.tensor_reduce(
+            out=res_view[:, 1, :],
+            in_=prod_a[:].rearrange("p r j a -> p (r j) a"),
+            axis=AXIS_X,
+            op=ADD,
+        )
 
         resT = keep.tile([P, Z_ROWS], F32, align_bytes=64)
         for i in OUTPUT_ORDER:

@@ -28,10 +28,10 @@ N_TILES = B // P
 Z_ROWS = ORD * R * N_TILES
 BLOCK = 32
 HALF = 256
-TILE_ORDER = (0, 3, 1, 2)
-SHARED, SCALAR = 0, 3
-VECTOR = (1, 2)
-OUTPUT_ORDER = (0, 2, 1)
+TILE_ORDER = (0, 1, 3, 2)
+SCALAR, SHARED = 0, 1
+VECTOR = (2, 3)
+OUTPUT_ORDER = (1, 0, 2)
 WARM = 4
 
 FLOPS = 2 * Q * KRON * B + 2 * 2 * KRON * B + 3 * 2 * RR * B
@@ -147,11 +147,12 @@ def tile_fast_tucker_taylor_pa_s_kernel(tc, z, G2, grad_out, out):
         mx_pass(3, 0)
         quantise("w", 1, 0, HALF)
         quantise("w", 1, HALF, 2 * HALF)
-        regroup(vector_copy, "g", 1, P, HALF)
-        regroup(vector_copy, "g", 1, HALF, HALF + P)
         regroup(scalar_copy, "g", 1, 0, P)
         regroup(scalar_copy, "g", 1, HALF + P, 2 * HALF)
+        regroup(vector_copy, "g", 1, P, HALF)
         for j in TILE_ORDER:
+            if j == TILE_ORDER[2]:
+                regroup(vector_copy, "g", 1, HALF, HALF + P)
             quantise("g", 1, j * P, (j + 1) * P)
             mx_pass(j, 1)
 
@@ -163,24 +164,24 @@ def tile_fast_tucker_taylor_pa_s_kernel(tc, z, G2, grad_out, out):
             return d_term, zT[:, 0, j, s : s + 1]
 
         nc.vector.tensor_tensor(
-            out=terms[:, 0, :, 0, :].rearrange("p c (a b) -> p c a b", b=R),
+            out=terms[:, SHARED, :, 0, :].rearrange("p c (a b) -> p c a b", b=R),
             in0=dT[SHARED][:].rearrange("p (c b a) -> p c a b", b=R, a=R),
             in1=zT[:, 2, SHARED, :].unsqueeze(2).unsqueeze(3).to_broadcast([P, R, R, R]),
             op=MULT,
         )
-        for slot, j, kinds in ((1, SCALAR, (0, 1)), (0, SHARED, (1,))):
+        for j, kinds in ((SCALAR, (0, 1)), (SHARED, (1,))):
             for s in range(R):
                 for k in kinds:
                     d_term, z_column = d_slice(j, s, k)
                     nc.scalar.activation(
-                        out=terms[:, slot, s, k, :].rearrange("p (y b) -> p y b", b=R),
+                        out=terms[:, j, s, k, :].rearrange("p (y b) -> p y b", b=R),
                         in_=d_term,
                         func=COPY,
                         scale=z_column,
                     )
                 nc.tensor.matmul(
-                    out=turned_ps[:, slot, :],
-                    lhsT=terms[:, slot, s, :, :].rearrange("p k x -> p (k x)"),
+                    out=turned_ps[:, j, :],
+                    lhsT=terms[:, j, s, :, :].rearrange("p k x -> p (k x)"),
                     rhs=ident_f32[:],
                     is_transpose=True,
                     start=(s == 0),
@@ -213,30 +214,30 @@ def tile_fast_tucker_taylor_pa_s_kernel(tc, z, G2, grad_out, out):
 
         def multiply(tiles, sums):
             nc.vector.tensor_tensor(
-                out=prod_b[:, :, tiles, :],
-                in0=sums.rearrange("p j (y b) -> p y j b", b=R),
-                in1=zT[:, 1, tiles, :].unsqueeze(1).to_broadcast([P, 2 * R, 2, R]),
-                op=MULT,
-            )
-            nc.vector.tensor_tensor(
                 out=prod_a[:, :, tiles, :],
                 in0=sums[:, :, 0:RR].rearrange("p j (a b) -> p b j a", b=R),
                 in1=zT[:, 0, tiles, :].unsqueeze(1).to_broadcast([P, R, 2, R]),
                 op=MULT,
             )
+            nc.vector.tensor_tensor(
+                out=prod_b[:, :, tiles, :],
+                in0=sums.rearrange("p j (y b) -> p y j b", b=R),
+                in1=zT[:, 1, tiles, :].unsqueeze(1).to_broadcast([P, 2 * R, 2, R]),
+                op=MULT,
+            )
 
-        multiply(slice(1, SCALAR), tu[:].rearrange("p j k x -> p j (k x)"))
-        multiply(slice(SHARED, N_TILES, SCALAR), small_ps[:, 1:3, :])
+        multiply(slice(2, N_TILES), tu[:].rearrange("p j k x -> p j (k x)"))
+        multiply(slice(0, 2), small_ps[:, 1:3, :])
         res_view = res[:].rearrange("p (i x) -> p i x", i=ORD)
         nc.vector.tensor_reduce(
-            out=res_view[:, 0:ORD:2, :],
-            in_=prod_b[:].rearrange("p (k r) j b -> p k (r j) b", k=2),
+            out=res_view[:, 1, :],
+            in_=prod_a[:].rearrange("p r j a -> p (r j) a"),
             axis=AXIS_X,
             op=ADD,
         )
         nc.vector.tensor_reduce(
-            out=res_view[:, 1, :],
-            in_=prod_a[:].rearrange("p r j a -> p (r j) a"),
+            out=res_view[:, 0:ORD:2, :],
+            in_=prod_b[:].rearrange("p (k r) j b -> p k (r j) b", k=2),
             axis=AXIS_X,
             op=ADD,
         )

@@ -32,6 +32,7 @@ TILE_ORDER = (0, 1, 3, 2)
 SCALAR, SHARED = 0, 1
 VECTOR = (2, 3)
 OUTPUT_ORDER = (1, 0, 2)
+RUN = 4
 WARM = 4
 
 FLOPS = 2 * Q * KRON * B + 2 * 2 * KRON * B + 3 * 2 * RR * B
@@ -97,8 +98,8 @@ def tile_fast_tucker_taylor_pa_s_kernel(tc, z, G2, grad_out, out):
 
         def regroup(copy, label, c, first, last):
             copy(
-                out=grouped[label][:, c, first:last, :],
-                in_=raw[(label, c)][:, :, first:last].rearrange("p t w -> p w t"),
+                out=grouped[label][:, c, first:last, :].rearrange("p (x i) t -> p x t i", i=RUN),
+                in_=raw[(label, c)][:, :, first:last].rearrange("p t (x i) -> p x t i", i=RUN),
             )
 
         def quantise(label, c, first, last):

from contextlib import ExitStack

import concourse.mybir as mybir
from concourse.masks import make_identity

BF16 = mybir.dt.bfloat16
F32 = mybir.dt.float32
U32 = mybir.dt.uint32
U8 = mybir.dt.uint8
E4M3X4 = mybir.dt.float8_e4m3fn_x4
E5M2X4 = mybir.dt.float8_e5m2_x4
MULT = mybir.AluOpType.mult
ADD = mybir.AluOpType.add
AXIS_X = mybir.AxisListType.X
COPY = mybir.ActivationFunctionType.Copy

P = 128
PACK = 4
K_PASS = P * PACK
Q = 1024
PASSES = Q // K_PASS
ORD = 3
R = 8
RR = R * R
KRON = R * R * R
B = 512
N_TILES = B // P
Z_ROWS = ORD * R * N_TILES
BLOCK = 32
HALF = 256
TILE_ORDER = (0, 1, 3, 2)
SCALAR, SHARED = 0, 1
VECTOR = (2, 3)
OUTPUT_ORDER = (1, 0, 2)
RUN = 4
WARM = 4

FLOPS = 2 * Q * KRON * B + 2 * 2 * KRON * B + 3 * 2 * RR * B


def tile_fast_tucker_taylor_pa_s_kernel(tc, z, G2, grad_out, out):
    nc = tc.nc
    with ExitStack() as ctx:
        keep = ctx.enter_context(tc.tile_pool(name="keep", bufs=1))
        psum = ctx.enter_context(tc.psum_pool(name="psum", bufs=1))
        ctx.enter_context(tc.manual_schedule())

        z_rows = keep.tile([P, P], BF16)
        z_view = z.rearrange("i r (j n) -> (i r j) n", j=N_TILES)
        nc.scalar.dma_start(out=z_rows[0:64, :], in_=z_view[0:64, :])
        nc.scalar.dma_start(out=z_rows[64:Z_ROWS, :], in_=z_view[64:Z_ROWS, :])
        nc.vector.memset(z_rows[Z_ROWS:P, :], 0.0)
        ident_bf = keep.tile([P, P], BF16)
        make_identity(nc, ident_bf[:])
        ident_f32 = keep.tile([P, P], F32)
        make_identity(nc, ident_f32[:])
        res = keep.tile([P, Z_ROWS], F32, align_bytes=64)

        raw = {}
        for c in range(PASSES):
            for source, label in ((G2, "w"), (grad_out, "g")):
                loaded = keep.tile([P, PACK, 2 * HALF], BF16, name="raw_%s%d" % (label, c))
                nc.sync.dma_start(
                    out=loaded[:],
                    in_=source[c * K_PASS : (c + 1) * K_PASS, :].rearrange(
                        "(p t) w -> p t w", t=PACK
                    ),
                )
                raw[(label, c)] = loaded

        small_bf_ps = psum.tile([P, 2, P], BF16)
        small_ps = psum.tile([P, 3, P], F32)
        turned_ps = psum.tile([P, 2, P], F32)
        terms = keep.tile([P, 2, R, 2, RR], F32)
        nc.tensor.transpose(small_bf_ps[:, 0, :], raw[("w", 0)][:, 0, 0:P], ident_bf[:])
        zT_ps = small_bf_ps[:, 1, :]
        for i in range(WARM):
            nc.tensor.matmul(
                out=small_ps[:, 0, :], lhsT=ident_f32[:], rhs=ident_f32[:], start=True, stop=True
            )
            if i == 1:
                nc.tensor.transpose(zT_ps, z_rows[:], ident_bf[:])

        grouped = {}
        codes = {}
        scales = {}
        for label in ("w", "g"):
            grouped[label] = keep.tile(
                [P, PASSES, 2 * HALF, PACK], BF16, align_bytes=64, name="grouped_%s" % label
            )
            codes[label] = keep.tile(
                [P, PASSES, 2 * HALF], U32, align_bytes=64, name="codes_%s" % label
            )
            scales[label] = keep.tile(
                [P, PASSES, 2 * HALF], U8, align_bytes=64, name="scales_%s" % label
            )
        formats = {"w": E4M3X4, "g": E5M2X4}

        def regroup(copy, label, c, first, last):
            copy(
                out=grouped[label][:, c, first:last, :].rearrange("p (x i) t -> p x t i", i=RUN),
                in_=raw[(label, c)][:, :, first:last].rearrange("p t (x i) -> p x t i", i=RUN),
            )

        def quantise(label, c, first, last):
            nc.vector.quantize_mx(
                out=codes[label][:, c, first:last].bitcast(formats[label]),
                scales=scales[label][:, c, first:last],
                in_=grouped[label][:, c, first:last, :].rearrange("p w t -> p (w t)"),
            )

        dT = []
        for j in range(N_TILES):
            dT.append(psum.tile([P, KRON], F32, name="dT%d" % j))

        def mx_pass(j, c):
            samples = slice(j * P, (j + 1) * P)
            nc.tensor.matmul_mx(
                out=dT[j][:],
                lhsT=codes["g"][:, c, samples].bitcast(E5M2X4),
                lhsT_scale=scales["g"][:, c, samples],
                rhs=codes["w"][:, c, :].bitcast(E4M3X4),
                rhs_scale=scales["w"][:, c, :],
                start=(c == 0),
                stop=(c == PASSES - 1),
            )

        vector_copy = nc.vector.tensor_copy
        scalar_copy = nc.scalar.copy
        regroup(vector_copy, "w", 0, 0, HALF)
        regroup(vector_copy, "w", 0, HALF, HALF + P)
        regroup(scalar_copy, "w", 0, HALF + P, 2 * HALF)
        quantise("w", 0, 0, HALF)
        regroup(vector_copy, "g", 0, 0, HALF)
        regroup(scalar_copy, "g", 0, HALF, 2 * HALF)
        quantise("w", 0, HALF, 2 * HALF)
        quantise("g", 0, 0, HALF)
        mx_pass(0, 0)
        mx_pass(1, 0)
        regroup(vector_copy, "w", 1, 0, HALF)
        regroup(scalar_copy, "w", 1, HALF, 2 * HALF)
        zT = keep.tile([P, ORD, N_TILES, R], F32)
        nc.scalar.copy(
            out=zT[:], in_=zT_ps[:, 0:Z_ROWS].rearrange("p (i r j) -> p i j r", i=ORD, r=R)
        )
        quantise("g", 0, HALF, 2 * HALF)
        mx_pass(2, 0)
        mx_pass(3, 0)
        quantise("w", 1, 0, HALF)
        quantise("w", 1, HALF, 2 * HALF)
        regroup(scalar_copy, "g", 1, 0, P)
        regroup(scalar_copy, "g", 1, HALF + P, 2 * HALF)
        regroup(vector_copy, "g", 1, P, HALF)
        for j in TILE_ORDER:
            if j == TILE_ORDER[2]:
                regroup(vector_copy, "g", 1, HALF, HALF + P)
            quantise("g", 1, j * P, (j + 1) * P)
            mx_pass(j, 1)

        def d_slice(j, s, k):
            if k == 0:
                d_term = dT[j][:, s * RR : (s + 1) * RR].rearrange("p (b a) -> p a b", a=R)
                return d_term, zT[:, 2, j, s : s + 1]
            d_term = dT[j][:].rearrange("p (c b a) -> p c b a", b=R, a=R)[:, :, :, s]
            return d_term, zT[:, 0, j, s : s + 1]

        nc.vector.tensor_tensor(
            out=terms[:, SHARED, :, 0, :].rearrange("p c (a b) -> p c a b", b=R),
            in0=dT[SHARED][:].rearrange("p (c b a) -> p c a b", b=R, a=R),
            in1=zT[:, 2, SHARED, :].unsqueeze(2).unsqueeze(3).to_broadcast([P, R, R, R]),
            op=MULT,
        )
        for j, kinds in ((SCALAR, (0, 1)), (SHARED, (1,))):
            for s in range(R):
                for k in kinds:
                    d_term, z_column = d_slice(j, s, k)
                    nc.scalar.activation(
                        out=terms[:, j, s, k, :].rearrange("p (y b) -> p y b", b=R),
                        in_=d_term,
                        func=COPY,
                        scale=z_column,
                    )
                nc.tensor.matmul(
                    out=turned_ps[:, j, :],
                    lhsT=terms[:, j, s, :, :].rearrange("p k x -> p (k x)"),
                    rhs=ident_f32[:],
                    is_transpose=True,
                    start=(s == 0),
                    stop=(s == R - 1),
                )
        turned = keep.tile([P, 2, P], F32)
        nc.scalar.copy(out=turned[:], in_=turned_ps[:])
        for slot in range(2):
            nc.tensor.transpose(small_ps[:, 1 + slot, :], turned[:, slot, :], ident_f32[:])

        tu = keep.tile([P, 2, 2, RR], F32)

        def vector_step(slot, j, s, k):
            d_term, z_column = d_slice(j, s, k)
            total = tu[:, slot, k, :].rearrange("p (y b) -> p y b", b=R)
            if s == 0:
                nc.vector.tensor_scalar_mul(out=total, in0=d_term, scalar1=z_column)
            else:
                nc.vector.scalar_tensor_tensor(
                    out=total, in0=d_term, scalar=z_column, in1=total, op0=MULT, op1=ADD
                )

        for s in range(R):
            for k in range(2):
                for slot, j in enumerate(VECTOR):
                    vector_step(slot, j, s, k)

        prod_b = keep.tile([P, 2 * R, N_TILES, R], F32)
        prod_a = keep.tile([P, R, N_TILES, R], F32)

        def multiply(tiles, sums):
            nc.vector.tensor_tensor(
                out=prod_a[:, :, tiles, :],
                in0=sums[:, :, 0:RR].rearrange("p j (a b) -> p b j a", b=R),
                in1=zT[:, 0, tiles, :].unsqueeze(1).to_broadcast([P, R, 2, R]),
                op=MULT,
            )
            nc.vector.tensor_tensor(
                out=prod_b[:, :, tiles, :],
                in0=sums.rearrange("p j (y b) -> p y j b", b=R),
                in1=zT[:, 1, tiles, :].unsqueeze(1).to_broadcast([P, 2 * R, 2, R]),
                op=MULT,
            )

        multiply(slice(2, N_TILES), tu[:].rearrange("p j k x -> p j (k x)"))
        multiply(slice(0, 2), small_ps[:, 1:3, :])
        res_view = res[:].rearrange("p (i x) -> p i x", i=ORD)
        nc.vector.tensor_reduce(
            out=res_view[:, 1, :],
            in_=prod_a[:].rearrange("p r j a -> p (r j) a"),
            axis=AXIS_X,
            op=ADD,
        )
        nc.vector.tensor_reduce(
            out=res_view[:, 0:ORD:2, :],
            in_=prod_b[:].rearrange("p (k r) j b -> p k (r j) b", k=2),
            axis=AXIS_X,
            op=ADD,
        )

        resT = keep.tile([P, Z_ROWS], F32, align_bytes=64)
        for i in OUTPUT_ORDER:
            block = slice(i * BLOCK, (i + 1) * BLOCK)
            nc.vector.transpose(out=resT[:, block], in_=res[:, block])
        out_blocks = out.rearrange("i r (j n) -> (i r j) n", j=N_TILES).rearrange(
            "(F f) (Q q) -> Q f F q", f=BLOCK, q=BLOCK
        )
        for quadrant in range(P // BLOCK):
            queue = nc.sync if quadrant < 2 else nc.scalar
            queue.dma_start(
                out=out_blocks[quadrant],
                in_=resT[quadrant * BLOCK : (quadrant + 1) * BLOCK, :].rearrange(
                    "f (F q) -> f F q", q=BLOCK
                ),
            )
